import numpy as np
import ml_dtypes


def mxq(x, axis, fmt="e4m3"):
    dtype, down = {"e4m3": (ml_dtypes.float8_e4m3fn, 7), "e5m2": (ml_dtypes.float8_e5m2, 14)}[fmt]
    v = np.moveaxis(np.asarray(x, np.float32).astype(ml_dtypes.bfloat16).astype(np.float64), axis, -1)
    blocks = v.reshape(v.shape[:-1] + (-1, 32))
    amax = np.abs(blocks).max(-1, keepdims=True)
    byte = np.maximum(np.where(amax > 0, np.frexp(amax)[1] - 1 + 127, 0) - down, 1)
    scale = np.exp2(byte - 127.0)
    codes = (blocks / scale).astype(np.float32).astype(dtype).astype(np.float64)
    return np.moveaxis((codes * scale).reshape(v.shape), -1, axis)


WIDE = False


def mx_kscale(k):
    if not WIDE:
        return np.ones(k)
    levels = np.array([10, -10, 5, -5, 0])
    a = np.random.permutation(np.resize(levels, k // 512 * 4)).reshape(k // 512, 4)
    idx = np.arange(k)
    return np.exp2(a[idx // 512, idx % 128 // 32])


BF16 = ml_dtypes.bfloat16


def bf(x):
    return np.asarray(x, np.float32).astype(BF16)


def f64(x):
    return np.asarray(x).astype(np.float64)


E2M1 = np.array([0.0, 0.5, 1.0, 1.5, 2.0, 3.0, 4.0, 6.0, -0.0, -0.5, -1.0, -1.5, -2.0, -3.0, -4.0, -6.0])


def pack_weight(w, fmt):
    k, n = w.shape
    w = f64(bf(w)).reshape(k // 32, 32, n)
    amax = np.abs(w).max(1)
    if fmt == "e4m3":
        byte = np.frexp(amax)[1] - 1 + 127 - 7
    else:
        mant, ex = np.frexp(amax / 6.0)
        byte = np.where(mant > 0.5, ex, ex - 1) + 127
    byte = np.clip(np.where(amax > 0, byte, 1), 1, 254)
    scaled = (w * np.exp2(127.0 - byte)[:, None, :]).reshape(k, n).astype(np.float32)
    by_word = np.ascontiguousarray(scaled.reshape(k // 512, 128, 4, n).transpose(0, 1, 3, 2))
    if fmt == "e4m3":
        words = by_word.astype(ml_dtypes.float8_e4m3fn).view(np.uint8)
    else:
        c = by_word.astype(ml_dtypes.float4_e2m1fn).view(np.uint8) & 0xF
        words = c[..., 0::2] | (c[..., 1::2] << 4)
    return np.ascontiguousarray(words), np.ascontiguousarray(byte.astype(np.uint8).reshape(k // 512, 16, n))


def unpack_weight(words, scales, fmt):
    g, p, n, _ = words.shape
    if fmt == "e4m3":
        vals = np.ascontiguousarray(words).view(ml_dtypes.float8_e4m3fn).astype(np.float64)
    else:
        nib = np.empty((g, p, n, 4), np.uint8)
        nib[..., 0::2] = words & 0xF
        nib[..., 1::2] = words >> 4
        vals = E2M1[nib]
    vals = vals * np.repeat(np.exp2(scales.astype(np.float64) - 127.0), 8, axis=1)[..., None]
    return vals.transpose(0, 1, 3, 2).reshape(g * 512, n)

def pack4(w):
    words, scales = pack_weight(w, "e2m1")
    return words.reshape(words.shape[0], 128, -1), scales


def unpack4(words, scales):
    return unpack_weight(words.reshape(words.shape[0], 128, -1, 2), scales, "e2m1")


B, S, E, H, DH, ROT, MP = 2, 64, 8192, 8, 128, 32, 4
HD = H * DH
LOC = HD // MP


def rope_sincos():
    inv_freq = 1.0 / (10000.0 ** (np.arange(0, ROT, 2) / ROT))
    ang = np.arange(S)[:, None] * inv_freq[None, :]
    return np.sin(ang), np.cos(ang)


def apply_rope(x, sin, cos):
    sin2 = np.repeat(sin, 2, axis=-1)[None, :, None, :]
    cos2 = np.repeat(cos, 2, axis=-1)[None, :, None, :]
    x1 = x[..., ::2]
    x2 = x[..., 1::2]
    rot = np.stack((-x2, x1), axis=-1).reshape(x.shape)
    return x * cos2 + rot * sin2


def setup_inputs():
    s = mx_kscale(E)
    hidden_states = bf(np.random.standard_normal((B, S, E)) * s)
    w = np.random.standard_normal((3 * HD, E)) / np.sqrt(E) / s[None, :]
    words, scales = pack4(np.ascontiguousarray(w.T))
    return {"hidden_states": hidden_states,
            "W_qkv_words": words,
            "W_qkv_scales": scales}


def reference(hidden_states, W_qkv_words, W_qkv_scales):
    qkv = mxq(f64(hidden_states), 2, "e4m3") @ unpack4(W_qkv_words, W_qkv_scales)
    qkv = qkv.reshape(B, S, MP, 3 * LOC)
    q, k, v = np.split(qkv, 3, axis=-1)
    q = q.reshape(B, S, H, DH)
    k = k.reshape(B, S, H, DH)
    v = v.reshape(B, S, H, DH)
    sin, cos = rope_sincos()
    q = np.concatenate([apply_rope(q[..., :ROT], sin, cos), q[..., ROT:]], axis=-1)
    k = np.concatenate([apply_rope(k[..., :ROT], sin, cos), k[..., ROT:]], axis=-1)
    return q, k, v

@@ -1,0 +1,251 @@
+import math
+
+import concourse.mybir as mybir
+from concourse.masks import make_identity
+
+F32 = mybir.dt.float32
+BF16 = mybir.dt.bfloat16
+I32 = mybir.dt.int32
+U32 = mybir.dt.uint32
+U8 = mybir.dt.uint8
+FP8X4 = mybir.dt.float8_e4m3fn_x4
+FP4X4 = mybir.dt.float4_e2m1fn_x4
+ALU = mybir.AluOpType
+ACT = mybir.ActivationFunctionType
+
+P = 128
+POSITIONS = 64
+K = 8192
+K_PASS = 512
+K_GROUPS = K // K_PASS
+N = 3072
+BANK = 512
+BANKS = N // BANK
+WIDE_BANKS = BANKS - 1
+WIDE = WIDE_BANKS * BANK
+FP4_BYTES = 2
+
+KINDS = 3
+BLOCK = 256
+COLUMN_GROUPS = N // (KINDS * BLOCK)
+HEAD = 128
+ROT = 32
+PAIRS = ROT // 2
+DOUBLINGS = 4
+HEADS = COLUMN_GROUPS * BLOCK // HEAD
+
+SCALE_RUNS = 2
+PLANE_GROUPS = 4
+NARROW_GROUPS = 4
+X_LOADS = 4
+
+ROUND_MAGIC = 12582912.0
+
+FLOPS = 2 * P * K * N
+
+assert 2**DOUBLINGS == PAIRS
+
+
+def tile_progenattention_pa_k_kernel(
+    tc, hidden_states, W_qkv_words, W_qkv_scales, out_0, out_1, out_2
+):
+    nc = tc.nc
+    x_dram = hidden_states.flatten_outer_dims()
+    word_ints = W_qkv_words.bitcast(I32)
+    scale_ints = W_qkv_scales.bitcast(I32)
+    outs = [o.rearrange("b s h d -> (b s) (h d)") for o in (out_0, out_1, out_2)]
+
+    with tc.tile_pool(name="keep", bufs=1) as keep, tc.tile_pool(
+        name="work", bufs=2
+    ) as work, tc.psum_pool(name="turn", bufs=2) as turn, tc.psum_pool(
+        name="sums", bufs=1
+    ) as sums, tc.manual_schedule():
+        x_sb = keep.tile([P, K], BF16, name="x_sb")
+        x_codes = keep.tile([P, K_GROUPS * P], U32, name="x_codes", align_bytes=64)
+        x_scales = keep.tile([P, K_GROUPS * P], U8, name="x_scales", align_bytes=64)
+        wide_words = [
+            keep.tile([P, WIDE * FP4_BYTES], U8, name="wide_words%d" % g, align_bytes=64)
+            for g in range(K_GROUPS)
+        ]
+        narrow_words = [
+            keep.tile(
+                [P, NARROW_GROUPS, BANK * FP4_BYTES], U8, name="narrow_words%d" % c, align_bytes=64
+            )
+            for c in range(K_GROUPS // NARROW_GROUPS)
+        ]
+        planes = [
+            keep.tile([P, PLANE_GROUPS, N], U8, name="planes%d" % c, align_bytes=64)
+            for c in range(K_GROUPS // PLANE_GROUPS)
+        ]
+        identity = keep.tile([P, P], F32, name="identity")
+        angles = keep.tile([P, 2 * PAIRS], F32, name="angles")
+        turns = keep.tile([P, 2 * PAIRS], F32, name="turns")
+        reduced = keep.tile([P, 2 * PAIRS], F32, name="reduced")
+        sin_cos = keep.tile([P, 2 * PAIRS], F32, name="sin_cos")
+        minus_sin = keep.tile([P, PAIRS], F32, name="minus_sin")
+        result = keep.tile([P, KINDS, HEADS * HEAD], F32, name="result")
+        acc = [sums.tile([P, BANK], F32, name="acc%d" % n) for n in range(BANKS)]
+
+        make_identity(nc, identity[:])
+        for batch in range(P // POSITIONS):
+            nc.gpsimd.iota(
+                angles[batch * POSITIONS : (batch + 1) * POSITIONS, 0:1],
+                pattern=[[0, 1]],
+                base=0,
+                channel_multiplier=1,
+                allow_small_or_imprecise_dtypes=True,
+            )
+        for plane in planes:
+            nc.vector.memset(plane[:].bitcast(I32), 0)
+
+        x_piece = K // X_LOADS
+        for i in range(X_LOADS):
+            cols = slice(i * x_piece, (i + 1) * x_piece)
+            nc.sync.dma_start(out=x_sb[:, cols], in_=x_dram[:, cols])
+
+        groups_per_run = K_GROUPS // SCALE_RUNS
+        for run in range(SCALE_RUNS):
+            first = run * groups_per_run
+            for c in range(first // PLANE_GROUPS, (first + groups_per_run) // PLANE_GROUPS):
+                plane_ints = planes[c][:].bitcast(I32)
+                for q in range(8):
+                    nc.sync.dma_start(
+                        out=plane_ints[32 * (q // 4) + q % 4 : P : 64],
+                        in_=scale_ints[
+                            c * PLANE_GROUPS : (c + 1) * PLANE_GROUPS, q : 16 : 8, :
+                        ].rearrange("g h n -> h g n"),
+                    )
+            for g in range(first, first + groups_per_run):
+                nc.sync.dma_start(
+                    out=wide_words[g][:].bitcast(I32),
+                    in_=word_ints[g, :, 0 : WIDE * FP4_BYTES // 4],
+                )
+        for c in range(K_GROUPS // NARROW_GROUPS):
+            nc.sync.dma_start(
+                out=narrow_words[c][:].bitcast(I32),
+                in_=word_ints[
+                    c * NARROW_GROUPS : (c + 1) * NARROW_GROUPS, :, WIDE * FP4_BYTES // 4 :
+                ].rearrange("g p b -> p g b"),
+            )
+
+        x_words = x_sb[:].bitcast(F32)
+        words_per_group = K_PASS // 2
+        for pair in range(K_GROUPS // 2):
+            turned = turn.tile([P, 2, 2, P], F32, name="turned")
+            for i in range(2):
+                g = 2 * pair + i
+                for u in range(2):
+                    nc.tensor.transpose(
+                        turned[:, i, u, :],
+                        x_words[:, g * words_per_group + u : (g + 1) * words_per_group : 2],
+                        identity[:],
+                    )
+            grouped = work.tile([P, 2 * K_PASS], BF16, name="grouped", align_bytes=64)
+            grouped_words = grouped[:].bitcast(F32).rearrange("p (i t u) -> p i t u", i=2, u=2)
+            turned_view = turned[:].rearrange("p i u t -> p i t u")
+            if pair % 2 == 0:
+                nc.scalar.copy(out=grouped_words, in_=turned_view)
+            else:
+                nc.vector.tensor_copy(out=grouped_words, in_=turned_view)
+            cols = slice(2 * pair * P, (2 * pair + 2) * P)
+            nc.vector.quantize_mx(
+                out=x_codes[:, cols].bitcast(FP8X4), scales=x_scales[:, cols], in_=grouped[:]
+            )
+
+        ratio = 10000.0 ** (-2.0 / ROT)
+        for doubling in range(DOUBLINGS):
+            filled = 2**doubling
+            nc.vector.tensor_scalar(
+                out=angles[:, filled : 2 * filled],
+                in0=angles[:, 0:filled],
+                scalar1=ratio**filled,
+                scalar2=None,
+                op0=ALU.mult,
+            )
+        nc.vector.tensor_scalar(
+            out=angles[:, PAIRS:],
+            in0=angles[:, 0:PAIRS],
+            scalar1=math.pi / 2,
+            scalar2=None,
+            op0=ALU.add,
+        )
+        nc.vector.tensor_scalar(
+            out=turns[:],
+            in0=angles[:],
+            scalar1=1.0 / (2 * math.pi),
+            scalar2=ROUND_MAGIC,
+            op0=ALU.mult,
+            op1=ALU.add,
+        )
+        nc.vector.tensor_scalar(
+            out=turns[:],
+            in0=turns[:],
+            scalar1=ROUND_MAGIC,
+            scalar2=2 * math.pi,
+            op0=ALU.subtract,
+            op1=ALU.mult,
+        )
+        nc.vector.tensor_tensor(out=reduced[:], in0=angles[:], in1=turns[:], op=ALU.subtract)
+        nc.scalar.activation(out=sin_cos[:], in_=reduced[:], func=ACT.Sin)
+        nc.scalar.activation(out=minus_sin[:], in_=reduced[:, 0:PAIRS], func=ACT.Sin, scale=-1.0)
+
+        def multiply(g, n, words):
+            nc.tensor.matmul_mx(
+                out=acc[n][:],
+                lhsT=x_codes[:, g * P : (g + 1) * P].bitcast(FP8X4),
+                lhsT_scale=x_scales[:, g * P : (g + 1) * P],
+                rhs=words.bitcast(FP4X4),
+                rhs_scale=planes[g // PLANE_GROUPS][:, g % PLANE_GROUPS, n * BANK : (n + 1) * BANK],
+                start=(g == 0),
+                stop=(g == K_GROUPS - 1),
+            )
+
+        def empty_bank(n):
+            for half in range(BANK // BLOCK):
+                group, kind = divmod(n * (BANK // BLOCK) + half, KINDS)
+                target = result[:, kind, group * BLOCK : (group + 1) * BLOCK]
+                source = acc[n][:, half * BLOCK : (half + 1) * BLOCK]
+                if n % 2 == 0:
+                    nc.scalar.copy(out=target, in_=source)
+                else:
+                    nc.vector.tensor_copy(out=target, in_=source)
+
+        qk_heads = result[:, 0:2, :].rearrange("p k (h d) -> p (k h) d", d=HEAD)
+
+        def rotate(first_head, heads, label):
+            x = qk_heads[:, first_head : first_head + heads, 0:ROT].rearrange(
+                "p h (j e) -> p h j e", e=2
+            )
+            shape = [P, heads, PAIRS]
+            sin = sin_cos[:, 0:PAIRS].unsqueeze(1).to_broadcast(shape)
+            neg = minus_sin[:].unsqueeze(1).to_broadcast(shape)
+            cos = sin_cos[:, PAIRS:].unsqueeze(1).unsqueeze(3).to_broadcast(shape + [2])
+            straight = work.tile([P, heads, PAIRS, 2], F32, name="straight_" + label)
+            crossed = work.tile([P, 2, heads, PAIRS], F32, name="crossed_" + label)
+            nc.vector.tensor_tensor(out=straight[:], in0=x, in1=cos, op=ALU.mult)
+            nc.vector.tensor_tensor(out=crossed[:, 0], in0=x[:, :, :, 1], in1=neg, op=ALU.mult)
+            nc.vector.tensor_tensor(out=crossed[:, 1], in0=x[:, :, :, 0], in1=sin, op=ALU.mult)
+            nc.vector.tensor_tensor(
+                out=x, in0=straight[:], in1=crossed[:].rearrange("p e h j -> p h j e"), op=ALU.add
+            )
+
+        def store(kind, first_group, groups):
+            cols = slice(first_group * BLOCK, (first_group + groups) * BLOCK)
+            nc.sync.dma_start(out=outs[kind][:, cols], in_=result[:, kind, cols])
+
+        for g in range(K_GROUPS):
+            for n in range(WIDE_BANKS):
+                multiply(g, n, wide_words[g][:, n * BANK * FP4_BYTES : (n + 1) * BANK * FP4_BYTES])
+        for n in range(WIDE_BANKS):
+            empty_bank(n)
+        store(2, 0, COLUMN_GROUPS - 1)
+        rotate(0, 2 * HEADS - BLOCK // HEAD, "wide")
+        store(0, 0, COLUMN_GROUPS)
+        store(1, 0, COLUMN_GROUPS - 1)
+
+        for g in range(K_GROUPS):
+            multiply(g, WIDE_BANKS, narrow_words[g // NARROW_GROUPS][:, g % NARROW_GROUPS, :])
+        empty_bank(WIDE_BANKS)
+        store(2, COLUMN_GROUPS - 1, 1)
+        rotate(2 * HEADS - BLOCK // HEAD, BLOCK // HEAD, "narrow")
+        store(1, COLUMN_GROUPS - 1, 1)

@@ -32,11 +32,11 @@ HEAD = 128
 ROT = 32
 PAIRS = ROT // 2
 DOUBLINGS = 4
-HEADS = COLUMN_GROUPS * BLOCK // HEAD
+QK_HEADS = 2 * BLOCK // HEAD
 
 SCALE_RUNS = 2
 PLANE_GROUPS = 4
-NARROW_GROUPS = 4
+NARROW_GROUPS = 2
 X_LOADS = 4
 
 ROUND_MAGIC = 12582912.0
@@ -83,7 +83,8 @@ def tile_progenattention_pa_k_kernel(
         reduced = keep.tile([P, 2 * PAIRS], F32, name="reduced")
         sin_cos = keep.tile([P, 2 * PAIRS], F32, name="sin_cos")
         minus_sin = keep.tile([P, PAIRS], F32, name="minus_sin")
-        result = keep.tile([P, KINDS, HEADS * HEAD], F32, name="result")
+        cos_twice = keep.tile([P, PAIRS, 2], F32, name="cos_twice")
+        result = keep.tile([P, N], F32, name="result")
         acc = [sums.tile([P, BANK], F32, name="acc%d" % n) for n in range(BANKS)]
 
         make_identity(nc, identity[:])
@@ -188,6 +189,9 @@ def tile_progenattention_pa_k_kernel(
         nc.vector.tensor_tensor(out=reduced[:], in0=angles[:], in1=turns[:], op=ALU.subtract)
         nc.scalar.activation(out=sin_cos[:], in_=reduced[:], func=ACT.Sin)
         nc.scalar.activation(out=minus_sin[:], in_=reduced[:, 0:PAIRS], func=ACT.Sin, scale=-1.0)
+        nc.vector.tensor_copy(
+            out=cos_twice[:], in_=sin_cos[:, PAIRS:].unsqueeze(2).to_broadcast([P, PAIRS, 2])
+        )
 
         def multiply(g, n, words):
             nc.tensor.matmul_mx(
@@ -201,51 +205,58 @@ def tile_progenattention_pa_k_kernel(
             )
 
         def empty_bank(n):
-            for half in range(BANK // BLOCK):
-                group, kind = divmod(n * (BANK // BLOCK) + half, KINDS)
-                target = result[:, kind, group * BLOCK : (group + 1) * BLOCK]
-                source = acc[n][:, half * BLOCK : (half + 1) * BLOCK]
-                if n % 2 == 0:
-                    nc.scalar.copy(out=target, in_=source)
-                else:
-                    nc.vector.tensor_copy(out=target, in_=source)
+            cols = slice(n * BANK, (n + 1) * BANK)
+            if n % 2 == 0:
+                nc.scalar.copy(out=result[:, cols], in_=acc[n][:])
+            else:
+                nc.vector.tensor_copy(out=result[:, cols], in_=acc[n][:])
 
-        qk_heads = result[:, 0:2, :].rearrange("p k (h d) -> p (k h) d", d=HEAD)
+        blocks = result[:].rearrange("p (g k c) -> p g k c", k=KINDS, c=BLOCK)
 
-        def rotate(first_head, heads, label):
-            x = qk_heads[:, first_head : first_head + heads, 0:ROT].rearrange(
-                "p h (j e) -> p h j e", e=2
+        def rotate(first_group, groups, label):
+            x = (
+                blocks[:, first_group : first_group + groups, 0:2, :]
+                .rearrange("p g k (h d) -> p g (k h) d", d=HEAD)[:, :, :, 0:ROT]
+                .rearrange("p g h (j e) -> p g h j e", e=2)
             )
-            shape = [P, heads, PAIRS]
-            sin = sin_cos[:, 0:PAIRS].unsqueeze(1).to_broadcast(shape)
-            neg = minus_sin[:].unsqueeze(1).to_broadcast(shape)
-            cos = sin_cos[:, PAIRS:].unsqueeze(1).unsqueeze(3).to_broadcast(shape + [2])
-            straight = work.tile([P, heads, PAIRS, 2], F32, name="straight_" + label)
-            crossed = work.tile([P, 2, heads, PAIRS], F32, name="crossed_" + label)
+            shape = [P, groups, QK_HEADS, PAIRS]
+            sin = sin_cos[:, 0:PAIRS].unsqueeze(1).unsqueeze(1).to_broadcast(shape)
+            neg = minus_sin[:].unsqueeze(1).unsqueeze(1).to_broadcast(shape)
+            cos = cos_twice[:].unsqueeze(1).unsqueeze(1).to_broadcast(shape + [2])
+            straight = work.tile(shape + [2], F32, name="straight_" + label)
+            crossed = work.tile([P, 2] + shape[1:], F32, name="crossed_" + label)
             nc.vector.tensor_tensor(out=straight[:], in0=x, in1=cos, op=ALU.mult)
-            nc.vector.tensor_tensor(out=crossed[:, 0], in0=x[:, :, :, 1], in1=neg, op=ALU.mult)
-            nc.vector.tensor_tensor(out=crossed[:, 1], in0=x[:, :, :, 0], in1=sin, op=ALU.mult)
+            nc.vector.tensor_tensor(out=crossed[:, 0], in0=x[:, :, :, :, 1], in1=neg, op=ALU.mult)
+            nc.vector.tensor_tensor(out=crossed[:, 1], in0=x[:, :, :, :, 0], in1=sin, op=ALU.mult)
             nc.vector.tensor_tensor(
-                out=x, in0=straight[:], in1=crossed[:].rearrange("p e h j -> p h j e"), op=ALU.add
+                out=x, in0=straight[:], in1=crossed[:].rearrange("p e g h j -> p g h j e"), op=ALU.add
             )
 
         def store(kind, first_group, groups):
-            cols = slice(first_group * BLOCK, (first_group + groups) * BLOCK)
-            nc.sync.dma_start(out=outs[kind][:, cols], in_=result[:, kind, cols])
+            nc.sync.dma_start(
+                out=outs[kind][:, first_group * BLOCK : (first_group + groups) * BLOCK].rearrange(
+                    "p (g c) -> p g c", c=BLOCK
+                ),
+                in_=blocks[:, first_group : first_group + groups, kind, :],
+            )
+
+        Q, KEY, V = range(KINDS)
+        done_wide = COLUMN_GROUPS - 1
 
         for g in range(K_GROUPS):
             for n in range(WIDE_BANKS):
                 multiply(g, n, wide_words[g][:, n * BANK * FP4_BYTES : (n + 1) * BANK * FP4_BYTES])
         for n in range(WIDE_BANKS):
             empty_bank(n)
-        store(2, 0, COLUMN_GROUPS - 1)
-        rotate(0, 2 * HEADS - BLOCK // HEAD, "wide")
-        store(0, 0, COLUMN_GROUPS)
-        store(1, 0, COLUMN_GROUPS - 1)
+        store(V, 0, done_wide)
+        rotate(0, done_wide, "wide")
+        store(Q, 0, done_wide)
+        store(KEY, 0, done_wide)
 
         for g in range(K_GROUPS):
             multiply(g, WIDE_BANKS, narrow_words[g // NARROW_GROUPS][:, g % NARROW_GROUPS, :])
         empty_bank(WIDE_BANKS)
-        store(2, COLUMN_GROUPS - 1, 1)
-        rotate(2 * HEADS - BLOCK // HEAD, BLOCK // HEAD, "narrow")
-        store(1, COLUMN_GROUPS - 1, 1)
+        store(V, done_wide, 1)
+        rotate(done_wide, 1, "narrow")
+        store(Q, done_wide, 1)
+        store(KEY, done_wide, 1)

@@ -32,11 +32,11 @@ HEAD = 128
 ROT = 32
 PAIRS = ROT // 2
 DOUBLINGS = 4
-QK_HEADS = 2 * BLOCK // HEAD
+HEADS = COLUMN_GROUPS * BLOCK // HEAD
 
-SCALE_RUNS = 2
+SCALE_RUNS = 1
 PLANE_GROUPS = 4
-NARROW_GROUPS = 2
+NARROW_GROUPS = 4
 X_LOADS = 4
 
 ROUND_MAGIC = 12582912.0
@@ -83,8 +83,7 @@ def tile_progenattention_pa_k_kernel(
         reduced = keep.tile([P, 2 * PAIRS], F32, name="reduced")
         sin_cos = keep.tile([P, 2 * PAIRS], F32, name="sin_cos")
         minus_sin = keep.tile([P, PAIRS], F32, name="minus_sin")
-        cos_twice = keep.tile([P, PAIRS, 2], F32, name="cos_twice")
-        result = keep.tile([P, N], F32, name="result")
+        result = keep.tile([P, KINDS, HEADS * HEAD], F32, name="result")
         acc = [sums.tile([P, BANK], F32, name="acc%d" % n) for n in range(BANKS)]
 
         make_identity(nc, identity[:])
@@ -189,9 +188,6 @@ def tile_progenattention_pa_k_kernel(
         nc.vector.tensor_tensor(out=reduced[:], in0=angles[:], in1=turns[:], op=ALU.subtract)
         nc.scalar.activation(out=sin_cos[:], in_=reduced[:], func=ACT.Sin)
         nc.scalar.activation(out=minus_sin[:], in_=reduced[:, 0:PAIRS], func=ACT.Sin, scale=-1.0)
-        nc.vector.tensor_copy(
-            out=cos_twice[:], in_=sin_cos[:, PAIRS:].unsqueeze(2).to_broadcast([P, PAIRS, 2])
-        )
 
         def multiply(g, n, words):
             nc.tensor.matmul_mx(
@@ -205,58 +201,51 @@ def tile_progenattention_pa_k_kernel(
             )
 
         def empty_bank(n):
-            cols = slice(n * BANK, (n + 1) * BANK)
-            if n % 2 == 0:
-                nc.scalar.copy(out=result[:, cols], in_=acc[n][:])
-            else:
-                nc.vector.tensor_copy(out=result[:, cols], in_=acc[n][:])
+            for half in range(BANK // BLOCK):
+                group, kind = divmod(n * (BANK // BLOCK) + half, KINDS)
+                target = result[:, kind, group * BLOCK : (group + 1) * BLOCK]
+                source = acc[n][:, half * BLOCK : (half + 1) * BLOCK]
+                if n % 2 == 0:
+                    nc.scalar.copy(out=target, in_=source)
+                else:
+                    nc.vector.tensor_copy(out=target, in_=source)
 
-        blocks = result[:].rearrange("p (g k c) -> p g k c", k=KINDS, c=BLOCK)
+        qk_heads = result[:, 0:2, :].rearrange("p k (h d) -> p (k h) d", d=HEAD)
 
-        def rotate(first_group, groups, label):
-            x = (
-                blocks[:, first_group : first_group + groups, 0:2, :]
-                .rearrange("p g k (h d) -> p g (k h) d", d=HEAD)[:, :, :, 0:ROT]
-                .rearrange("p g h (j e) -> p g h j e", e=2)
+        def rotate(first_head, heads, label):
+            x = qk_heads[:, first_head : first_head + heads, 0:ROT].rearrange(
+                "p h (j e) -> p h j e", e=2
             )
-            shape = [P, groups, QK_HEADS, PAIRS]
-            sin = sin_cos[:, 0:PAIRS].unsqueeze(1).unsqueeze(1).to_broadcast(shape)
-            neg = minus_sin[:].unsqueeze(1).unsqueeze(1).to_broadcast(shape)
-            cos = cos_twice[:].unsqueeze(1).unsqueeze(1).to_broadcast(shape + [2])
-            straight = work.tile(shape + [2], F32, name="straight_" + label)
-            crossed = work.tile([P, 2] + shape[1:], F32, name="crossed_" + label)
+            shape = [P, heads, PAIRS]
+            sin = sin_cos[:, 0:PAIRS].unsqueeze(1).to_broadcast(shape)
+            neg = minus_sin[:].unsqueeze(1).to_broadcast(shape)
+            cos = sin_cos[:, PAIRS:].unsqueeze(1).unsqueeze(3).to_broadcast(shape + [2])
+            straight = work.tile([P, heads, PAIRS, 2], F32, name="straight_" + label)
+            crossed = work.tile([P, 2, heads, PAIRS], F32, name="crossed_" + label)
             nc.vector.tensor_tensor(out=straight[:], in0=x, in1=cos, op=ALU.mult)
-            nc.vector.tensor_tensor(out=crossed[:, 0], in0=x[:, :, :, :, 1], in1=neg, op=ALU.mult)
-            nc.vector.tensor_tensor(out=crossed[:, 1], in0=x[:, :, :, :, 0], in1=sin, op=ALU.mult)
+            nc.vector.tensor_tensor(out=crossed[:, 0], in0=x[:, :, :, 1], in1=neg, op=ALU.mult)
+            nc.vector.tensor_tensor(out=crossed[:, 1], in0=x[:, :, :, 0], in1=sin, op=ALU.mult)
             nc.vector.tensor_tensor(
-                out=x, in0=straight[:], in1=crossed[:].rearrange("p e g h j -> p g h j e"), op=ALU.add
+                out=x, in0=straight[:], in1=crossed[:].rearrange("p e h j -> p h j e"), op=ALU.add
             )
 
         def store(kind, first_group, groups):
-            nc.sync.dma_start(
-                out=outs[kind][:, first_group * BLOCK : (first_group + groups) * BLOCK].rearrange(
-                    "p (g c) -> p g c", c=BLOCK
-                ),
-                in_=blocks[:, first_group : first_group + groups, kind, :],
-            )
-
-        Q, KEY, V = range(KINDS)
-        done_wide = COLUMN_GROUPS - 1
+            cols = slice(first_group * BLOCK, (first_group + groups) * BLOCK)
+            nc.sync.dma_start(out=outs[kind][:, cols], in_=result[:, kind, cols])
 
         for g in range(K_GROUPS):
             for n in range(WIDE_BANKS):
                 multiply(g, n, wide_words[g][:, n * BANK * FP4_BYTES : (n + 1) * BANK * FP4_BYTES])
         for n in range(WIDE_BANKS):
             empty_bank(n)
-        store(V, 0, done_wide)
-        rotate(0, done_wide, "wide")
-        store(Q, 0, done_wide)
-        store(KEY, 0, done_wide)
+        store(2, 0, COLUMN_GROUPS - 1)
+        rotate(0, 2 * HEADS - BLOCK // HEAD, "wide")
+        store(0, 0, COLUMN_GROUPS)
+        store(1, 0, COLUMN_GROUPS - 1)
 
         for g in range(K_GROUPS):
             multiply(g, WIDE_BANKS, narrow_words[g // NARROW_GROUPS][:, g % NARROW_GROUPS, :])
         empty_bank(WIDE_BANKS)
-        store(V, done_wide, 1)
-        rotate(done_wide, 1, "narrow")
-        store(Q, done_wide, 1)
-        store(KEY, done_wide, 1)
+        store(2, COLUMN_GROUPS - 1, 1)
+        rotate(2 * HEADS - BLOCK // HEAD, BLOCK // HEAD, "narrow")
+        store(1, COLUMN_GROUPS - 1, 1)

@@ -35,7 +35,7 @@ DOUBLINGS = 4
 HEADS = COLUMN_GROUPS * BLOCK // HEAD
 
 SCALE_RUNS = 1
-PLANE_GROUPS = 4
+PLANE_GROUPS = 8
 NARROW_GROUPS = 4
 X_LOADS = 4
 

@@ -34,8 +34,7 @@ PAIRS = ROT // 2
 DOUBLINGS = 4
 HEADS = COLUMN_GROUPS * BLOCK // HEAD
 
-SCALE_RUNS = 1
-PLANE_GROUPS = 8
+SCALE_ROWS = 16
 NARROW_GROUPS = 4
 X_LOADS = 4
 
@@ -73,10 +72,7 @@ def tile_progenattention_pa_k_kernel(
             )
             for c in range(K_GROUPS // NARROW_GROUPS)
         ]
-        planes = [
-            keep.tile([P, PLANE_GROUPS, N], U8, name="planes%d" % c, align_bytes=64)
-            for c in range(K_GROUPS // PLANE_GROUPS)
-        ]
+        planes = keep.tile([P, K_GROUPS, N], U8, name="planes", align_bytes=64)
         identity = keep.tile([P, P], F32, name="identity")
         angles = keep.tile([P, 2 * PAIRS], F32, name="angles")
         turns = keep.tile([P, 2 * PAIRS], F32, name="turns")
@@ -95,31 +91,29 @@ def tile_progenattention_pa_k_kernel(
                 channel_multiplier=1,
                 allow_small_or_imprecise_dtypes=True,
             )
-        for plane in planes:
-            nc.vector.memset(plane[:].bitcast(I32), 0)
+        nc.vector.memset(planes[:].bitcast(I32), 0)
 
         x_piece = K // X_LOADS
         for i in range(X_LOADS):
             cols = slice(i * x_piece, (i + 1) * x_piece)
             nc.sync.dma_start(out=x_sb[:, cols], in_=x_dram[:, cols])
 
-        groups_per_run = K_GROUPS // SCALE_RUNS
-        for run in range(SCALE_RUNS):
-            first = run * groups_per_run
-            for c in range(first // PLANE_GROUPS, (first + groups_per_run) // PLANE_GROUPS):
-                plane_ints = planes[c][:].bitcast(I32)
-                for q in range(8):
-                    nc.sync.dma_start(
-                        out=plane_ints[32 * (q // 4) + q % 4 : P : 64],
-                        in_=scale_ints[
-                            c * PLANE_GROUPS : (c + 1) * PLANE_GROUPS, q : 16 : 8, :
-                        ].rearrange("g h n -> h g n"),
-                    )
-            for g in range(first, first + groups_per_run):
+        def load_wide(g):
+            nc.sync.dma_start(
+                out=wide_words[g][:].bitcast(I32), in_=word_ints[g, :, 0 : WIDE * FP4_BYTES // 4]
+            )
+
+        load_wide(0)
+        plane_ints = planes[:].bitcast(I32)
+        for low in range(SCALE_ROWS // 2):
+            for q in (low, low + SCALE_ROWS // 2):
+                partition = 32 * (q // 4) + q % 4
                 nc.sync.dma_start(
-                    out=wide_words[g][:].bitcast(I32),
-                    in_=word_ints[g, :, 0 : WIDE * FP4_BYTES // 4],
+                    out=plane_ints[partition : partition + 1],
+                    in_=scale_ints[:, q : q + 1, :].rearrange("g o n -> o g n"),
                 )
+        for g in range(1, K_GROUPS):
+            load_wide(g)
         for c in range(K_GROUPS // NARROW_GROUPS):
             nc.sync.dma_start(
                 out=narrow_words[c][:].bitcast(I32),
@@ -195,7 +189,7 @@ def tile_progenattention_pa_k_kernel(
                 lhsT=x_codes[:, g * P : (g + 1) * P].bitcast(FP8X4),
                 lhsT_scale=x_scales[:, g * P : (g + 1) * P],
                 rhs=words.bitcast(FP4X4),
-                rhs_scale=planes[g // PLANE_GROUPS][:, g % PLANE_GROUPS, n * BANK : (n + 1) * BANK],
+                rhs_scale=planes[:, g, n * BANK : (n + 1) * BANK],
                 start=(g == 0),
                 stop=(g == K_GROUPS - 1),
             )

@@ -35,7 +35,7 @@ DOUBLINGS = 4
 HEADS = COLUMN_GROUPS * BLOCK // HEAD
 
 SCALE_ROWS = 16
-NARROW_GROUPS = 4
+NARROW_LOADS = (4, 4, 4, 2, 1, 1)
 X_LOADS = 4
 
 ROUND_MAGIC = 12582912.0
@@ -43,6 +43,7 @@ ROUND_MAGIC = 12582912.0
 FLOPS = 2 * P * K * N
 
 assert 2**DOUBLINGS == PAIRS
+assert sum(NARROW_LOADS) == K_GROUPS
 
 
 def tile_progenattention_pa_k_kernel(
@@ -67,18 +68,16 @@ def tile_progenattention_pa_k_kernel(
             for g in range(K_GROUPS)
         ]
         narrow_words = [
-            keep.tile(
-                [P, NARROW_GROUPS, BANK * FP4_BYTES], U8, name="narrow_words%d" % c, align_bytes=64
-            )
-            for c in range(K_GROUPS // NARROW_GROUPS)
+            keep.tile([P, groups, BANK * FP4_BYTES], U8, name="narrow_words%d" % c, align_bytes=64)
+            for c, groups in enumerate(NARROW_LOADS)
         ]
         planes = keep.tile([P, K_GROUPS, N], U8, name="planes", align_bytes=64)
         identity = keep.tile([P, P], F32, name="identity")
         angles = keep.tile([P, 2 * PAIRS], F32, name="angles")
         turns = keep.tile([P, 2 * PAIRS], F32, name="turns")
         reduced = keep.tile([P, 2 * PAIRS], F32, name="reduced")
-        sin_cos = keep.tile([P, 2 * PAIRS], F32, name="sin_cos")
-        minus_sin = keep.tile([P, PAIRS], F32, name="minus_sin")
+        cos = keep.tile([P, PAIRS], F32, name="cos")
+        sin = keep.tile([P, PAIRS, 2], F32, name="sin")
         result = keep.tile([P, KINDS, HEADS * HEAD], F32, name="result")
         acc = [sums.tile([P, BANK], F32, name="acc%d" % n) for n in range(BANKS)]
 
@@ -114,13 +113,16 @@ def tile_progenattention_pa_k_kernel(
                 )
         for g in range(1, K_GROUPS):
             load_wide(g)
-        for c in range(K_GROUPS // NARROW_GROUPS):
+        narrow_slices = []
+        for tile, groups in zip(narrow_words, NARROW_LOADS):
+            first = len(narrow_slices)
             nc.sync.dma_start(
-                out=narrow_words[c][:].bitcast(I32),
-                in_=word_ints[
-                    c * NARROW_GROUPS : (c + 1) * NARROW_GROUPS, :, WIDE * FP4_BYTES // 4 :
-                ].rearrange("g p b -> p g b"),
+                out=tile[:].bitcast(I32),
+                in_=word_ints[first : first + groups, :, WIDE * FP4_BYTES // 4 :].rearrange(
+                    "g p b -> p g b"
+                ),
             )
+            narrow_slices.extend([tile[:, i, :] for i in range(groups)])
 
         x_words = x_sb[:].bitcast(F32)
         words_per_group = K_PASS // 2
@@ -180,8 +182,11 @@ def tile_progenattention_pa_k_kernel(
             op1=ALU.mult,
         )
         nc.vector.tensor_tensor(out=reduced[:], in0=angles[:], in1=turns[:], op=ALU.subtract)
-        nc.scalar.activation(out=sin_cos[:], in_=reduced[:], func=ACT.Sin)
-        nc.scalar.activation(out=minus_sin[:], in_=reduced[:, 0:PAIRS], func=ACT.Sin, scale=-1.0)
+        nc.scalar.activation(out=cos[:], in_=reduced[:, PAIRS:], func=ACT.Sin)
+        nc.scalar.activation(out=sin[:, :, 0], in_=reduced[:, 0:PAIRS], func=ACT.Sin)
+        nc.scalar.activation(
+            out=sin[:, :, 1], in_=reduced[:, 0:PAIRS], func=ACT.Sin, scale=-1.0
+        )
 
         def multiply(g, n, words):
             nc.tensor.matmul_mx(
@@ -206,21 +211,29 @@ def tile_progenattention_pa_k_kernel(
 
         qk_heads = result[:, 0:2, :].rearrange("p k (h d) -> p (k h) d", d=HEAD)
 
-        def rotate(first_head, heads, label):
-            x = qk_heads[:, first_head : first_head + heads, 0:ROT].rearrange(
-                "p h (j e) -> p h j e", e=2
-            )
-            shape = [P, heads, PAIRS]
-            sin = sin_cos[:, 0:PAIRS].unsqueeze(1).to_broadcast(shape)
-            neg = minus_sin[:].unsqueeze(1).to_broadcast(shape)
-            cos = sin_cos[:, PAIRS:].unsqueeze(1).unsqueeze(3).to_broadcast(shape + [2])
-            straight = work.tile([P, heads, PAIRS, 2], F32, name="straight_" + label)
-            crossed = work.tile([P, 2, heads, PAIRS], F32, name="crossed_" + label)
-            nc.vector.tensor_tensor(out=straight[:], in0=x, in1=cos, op=ALU.mult)
-            nc.vector.tensor_tensor(out=crossed[:, 0], in0=x[:, :, :, 1], in1=neg, op=ALU.mult)
-            nc.vector.tensor_tensor(out=crossed[:, 1], in0=x[:, :, :, 0], in1=sin, op=ALU.mult)
+        def multiply_pairs(source, label):
+            heads = source.shape[1]
+            x = source[:, :, 0:ROT].rearrange("p h (j e) -> p h j e", e=2)
+            shape = [P, heads, PAIRS, 2]
+            straight = work.tile(shape, F32, name="straight_" + label)
+            crossed = work.tile(shape, F32, name="crossed_" + label)
             nc.vector.tensor_tensor(
-                out=x, in0=straight[:], in1=crossed[:].rearrange("p e h j -> p h j e"), op=ALU.add
+                out=straight[:],
+                in0=x,
+                in1=cos[:].unsqueeze(1).unsqueeze(3).to_broadcast(shape),
+                op=ALU.mult,
+            )
+            nc.vector.tensor_tensor(
+                out=crossed[:], in0=x, in1=sin[:].unsqueeze(1).to_broadcast(shape), op=ALU.mult
+            )
+            return straight, crossed
+
+        def add_pairs(target, straight, crossed):
+            nc.vector.tensor_tensor(
+                out=target[:, :, 0:ROT].rearrange("p h (j e) -> p h j e", e=2),
+                in0=straight[:],
+                in1=crossed[:, :, :, ::-1],
+                op=ALU.add,
             )
 
         def store(kind, first_group, groups):
@@ -233,13 +246,21 @@ def tile_progenattention_pa_k_kernel(
         for n in range(WIDE_BANKS):
             empty_bank(n)
         store(2, 0, COLUMN_GROUPS - 1)
-        rotate(0, 2 * HEADS - BLOCK // HEAD, "wide")
+        block_heads = BLOCK // HEAD
+        wide_heads = qk_heads[:, 0 : 2 * HEADS - block_heads, :]
+        straight, crossed = multiply_pairs(wide_heads, "wide")
+        add_pairs(wide_heads, straight, crossed)
         store(0, 0, COLUMN_GROUPS)
         store(1, 0, COLUMN_GROUPS - 1)
 
         for g in range(K_GROUPS):
-            multiply(g, WIDE_BANKS, narrow_words[g // NARROW_GROUPS][:, g % NARROW_GROUPS, :])
-        empty_bank(WIDE_BANKS)
-        store(2, COLUMN_GROUPS - 1, 1)
-        rotate(2 * HEADS - BLOCK // HEAD, BLOCK // HEAD, "narrow")
+            multiply(g, WIDE_BANKS, narrow_slices[g])
+        k_bank = acc[WIDE_BANKS][:, 0:BLOCK].rearrange("p (h d) -> p h d", d=HEAD)
+        k_heads = qk_heads[:, 2 * HEADS - block_heads :, :]
+        straight, crossed = multiply_pairs(k_bank, "narrow")
+        nc.vector.tensor_copy(out=k_heads[:, :, ROT:], in_=k_bank[:, :, ROT:])
+        add_pairs(k_heads, straight, crossed)
         store(1, COLUMN_GROUPS - 1, 1)
+        v_cols = slice((COLUMN_GROUPS - 1) * BLOCK, COLUMN_GROUPS * BLOCK)
+        nc.scalar.copy(out=result[:, 2, v_cols], in_=acc[WIDE_BANKS][:, BLOCK:])
+        nc.scalar.dma_start(out=outs[2][:, v_cols], in_=result[:, 2, v_cols])

import math

import concourse.mybir as mybir
from concourse.masks import make_identity

F32 = mybir.dt.float32
BF16 = mybir.dt.bfloat16
I32 = mybir.dt.int32
U32 = mybir.dt.uint32
U8 = mybir.dt.uint8
FP8X4 = mybir.dt.float8_e4m3fn_x4
FP4X4 = mybir.dt.float4_e2m1fn_x4
ALU = mybir.AluOpType
ACT = mybir.ActivationFunctionType

P = 128
POSITIONS = 64
K = 8192
K_PASS = 512
K_GROUPS = K // K_PASS
N = 3072
BANK = 512
BANKS = N // BANK
WIDE_BANKS = BANKS - 1
WIDE = WIDE_BANKS * BANK
FP4_BYTES = 2

KINDS = 3
BLOCK = 256
COLUMN_GROUPS = N // (KINDS * BLOCK)
HEAD = 128
ROT = 32
PAIRS = ROT // 2
DOUBLINGS = 4
HEADS = COLUMN_GROUPS * BLOCK // HEAD

SCALE_ROWS = 16
NARROW_LOADS = (4, 4, 4, 2, 1, 1)
X_LOADS = 4

ROUND_MAGIC = 12582912.0

FLOPS = 2 * P * K * N

assert 2**DOUBLINGS == PAIRS
assert sum(NARROW_LOADS) == K_GROUPS


def tile_progenattention_pa_k_kernel(
    tc, hidden_states, W_qkv_words, W_qkv_scales, out_0, out_1, out_2
):
    nc = tc.nc
    x_dram = hidden_states.flatten_outer_dims()
    word_ints = W_qkv_words.bitcast(I32)
    scale_ints = W_qkv_scales.bitcast(I32)
    outs = [o.rearrange("b s h d -> (b s) (h d)") for o in (out_0, out_1, out_2)]

    with tc.tile_pool(name="keep", bufs=1) as keep, tc.tile_pool(
        name="work", bufs=2
    ) as work, tc.psum_pool(name="turn", bufs=2) as turn, tc.psum_pool(
        name="sums", bufs=1
    ) as sums, tc.manual_schedule():
        x_sb = keep.tile([P, K], BF16, name="x_sb")
        x_codes = keep.tile([P, K_GROUPS * P], U32, name="x_codes", align_bytes=64)
        x_scales = keep.tile([P, K_GROUPS * P], U8, name="x_scales", align_bytes=64)
        wide_words = [
            keep.tile([P, WIDE * FP4_BYTES], U8, name="wide_words%d" % g, align_bytes=64)
            for g in range(K_GROUPS)
        ]
        narrow_words = [
            keep.tile([P, groups, BANK * FP4_BYTES], U8, name="narrow_words%d" % c, align_bytes=64)
            for c, groups in enumerate(NARROW_LOADS)
        ]
        planes = keep.tile([P, K_GROUPS, N], U8, name="planes", align_bytes=64)
        identity = keep.tile([P, P], F32, name="identity")
        angles = keep.tile([P, 2 * PAIRS], F32, name="angles")
        turns = keep.tile([P, 2 * PAIRS], F32, name="turns")
        reduced = keep.tile([P, 2 * PAIRS], F32, name="reduced")
        cos = keep.tile([P, PAIRS], F32, name="cos")
        sin = keep.tile([P, PAIRS, 2], F32, name="sin")
        result = keep.tile([P, KINDS, HEADS * HEAD], F32, name="result")
        acc = [sums.tile([P, BANK], F32, name="acc%d" % n) for n in range(BANKS)]

        make_identity(nc, identity[:])
        for batch in range(P // POSITIONS):
            nc.gpsimd.iota(
                angles[batch * POSITIONS : (batch + 1) * POSITIONS, 0:1],
                pattern=[[0, 1]],
                base=0,
                channel_multiplier=1,
                allow_small_or_imprecise_dtypes=True,
            )
        nc.vector.memset(planes[:].bitcast(I32), 0)

        x_piece = K // X_LOADS
        for i in range(X_LOADS):
            cols = slice(i * x_piece, (i + 1) * x_piece)
            nc.sync.dma_start(out=x_sb[:, cols], in_=x_dram[:, cols])

        def load_wide(g):
            nc.sync.dma_start(
                out=wide_words[g][:].bitcast(I32), in_=word_ints[g, :, 0 : WIDE * FP4_BYTES // 4]
            )

        load_wide(0)
        plane_ints = planes[:].bitcast(I32)
        for low in range(SCALE_ROWS // 2):
            for q in (low, low + SCALE_ROWS // 2):
                partition = 32 * (q // 4) + q % 4
                nc.sync.dma_start(
                    out=plane_ints[partition : partition + 1],
                    in_=scale_ints[:, q : q + 1, :].rearrange("g o n -> o g n"),
                )
        for g in range(1, K_GROUPS):
            load_wide(g)
        narrow_slices = []
        for tile, groups in zip(narrow_words, NARROW_LOADS):
            first = len(narrow_slices)
            nc.sync.dma_start(
                out=tile[:].bitcast(I32),
                in_=word_ints[first : first + groups, :, WIDE * FP4_BYTES // 4 :].rearrange(
                    "g p b -> p g b"
                ),
            )
            narrow_slices.extend([tile[:, i, :] for i in range(groups)])

        x_words = x_sb[:].bitcast(F32)
        words_per_group = K_PASS // 2
        for pair in range(K_GROUPS // 2):
            turned = turn.tile([P, 2, 2, P], F32, name="turned")
            for i in range(2):
                g = 2 * pair + i
                for u in range(2):
                    nc.tensor.transpose(
                        turned[:, i, u, :],
                        x_words[:, g * words_per_group + u : (g + 1) * words_per_group : 2],
                        identity[:],
                    )
            grouped = work.tile([P, 2 * K_PASS], BF16, name="grouped", align_bytes=64)
            grouped_words = grouped[:].bitcast(F32).rearrange("p (i t u) -> p i t u", i=2, u=2)
            turned_view = turned[:].rearrange("p i u t -> p i t u")
            if pair % 2 == 0:
                nc.scalar.copy(out=grouped_words, in_=turned_view)
            else:
                nc.vector.tensor_copy(out=grouped_words, in_=turned_view)
            cols = slice(2 * pair * P, (2 * pair + 2) * P)
            nc.vector.quantize_mx(
                out=x_codes[:, cols].bitcast(FP8X4), scales=x_scales[:, cols], in_=grouped[:]
            )

        ratio = 10000.0 ** (-2.0 / ROT)
        for doubling in range(DOUBLINGS):
            filled = 2**doubling
            nc.vector.tensor_scalar(
                out=angles[:, filled : 2 * filled],
                in0=angles[:, 0:filled],
                scalar1=ratio**filled,
                scalar2=None,
                op0=ALU.mult,
            )
        nc.vector.tensor_scalar(
            out=angles[:, PAIRS:],
            in0=angles[:, 0:PAIRS],
            scalar1=math.pi / 2,
            scalar2=None,
            op0=ALU.add,
        )
        nc.vector.tensor_scalar(
            out=turns[:],
            in0=angles[:],
            scalar1=1.0 / (2 * math.pi),
            scalar2=ROUND_MAGIC,
            op0=ALU.mult,
            op1=ALU.add,
        )
        nc.vector.tensor_scalar(
            out=turns[:],
            in0=turns[:],
            scalar1=ROUND_MAGIC,
            scalar2=2 * math.pi,
            op0=ALU.subtract,
            op1=ALU.mult,
        )
        nc.vector.tensor_tensor(out=reduced[:], in0=angles[:], in1=turns[:], op=ALU.subtract)
        nc.scalar.activation(out=cos[:], in_=reduced[:, PAIRS:], func=ACT.Sin)
        nc.scalar.activation(out=sin[:, :, 0], in_=reduced[:, 0:PAIRS], func=ACT.Sin)
        nc.scalar.activation(
            out=sin[:, :, 1], in_=reduced[:, 0:PAIRS], func=ACT.Sin, scale=-1.0
        )

        def multiply(g, n, words):
            nc.tensor.matmul_mx(
                out=acc[n][:],
                lhsT=x_codes[:, g * P : (g + 1) * P].bitcast(FP8X4),
                lhsT_scale=x_scales[:, g * P : (g + 1) * P],
                rhs=words.bitcast(FP4X4),
                rhs_scale=planes[:, g, n * BANK : (n + 1) * BANK],
                start=(g == 0),
                stop=(g == K_GROUPS - 1),
            )

        def empty_bank(n):
            for half in range(BANK // BLOCK):
                group, kind = divmod(n * (BANK // BLOCK) + half, KINDS)
                target = result[:, kind, group * BLOCK : (group + 1) * BLOCK]
                source = acc[n][:, half * BLOCK : (half + 1) * BLOCK]
                if n % 2 == 0:
                    nc.scalar.copy(out=target, in_=source)
                else:
                    nc.vector.tensor_copy(out=target, in_=source)

        qk_heads = result[:, 0:2, :].rearrange("p k (h d) -> p (k h) d", d=HEAD)

        def multiply_pairs(source, label):
            heads = source.shape[1]
            x = source[:, :, 0:ROT].rearrange("p h (j e) -> p h j e", e=2)
            shape = [P, heads, PAIRS, 2]
            straight = work.tile(shape, F32, name="straight_" + label)
            crossed = work.tile(shape, F32, name="crossed_" + label)
            nc.vector.tensor_tensor(
                out=straight[:],
                in0=x,
                in1=cos[:].unsqueeze(1).unsqueeze(3).to_broadcast(shape),
                op=ALU.mult,
            )
            nc.vector.tensor_tensor(
                out=crossed[:], in0=x, in1=sin[:].unsqueeze(1).to_broadcast(shape), op=ALU.mult
            )
            return straight, crossed

        def add_pairs(target, straight, crossed):
            nc.vector.tensor_tensor(
                out=target[:, :, 0:ROT].rearrange("p h (j e) -> p h j e", e=2),
                in0=straight[:],
                in1=crossed[:, :, :, ::-1],
                op=ALU.add,
            )

        def store(kind, first_group, groups):
            cols = slice(first_group * BLOCK, (first_group + groups) * BLOCK)
            nc.sync.dma_start(out=outs[kind][:, cols], in_=result[:, kind, cols])

        for g in range(K_GROUPS):
            for n in range(WIDE_BANKS):
                multiply(g, n, wide_words[g][:, n * BANK * FP4_BYTES : (n + 1) * BANK * FP4_BYTES])
        for n in range(WIDE_BANKS):
            empty_bank(n)
        store(2, 0, COLUMN_GROUPS - 1)
        block_heads = BLOCK // HEAD
        wide_heads = qk_heads[:, 0 : 2 * HEADS - block_heads, :]
        straight, crossed = multiply_pairs(wide_heads, "wide")
        add_pairs(wide_heads, straight, crossed)
        store(0, 0, COLUMN_GROUPS)
        store(1, 0, COLUMN_GROUPS - 1)

        for g in range(K_GROUPS):
            multiply(g, WIDE_BANKS, narrow_slices[g])
        k_bank = acc[WIDE_BANKS][:, 0:BLOCK].rearrange("p (h d) -> p h d", d=HEAD)
        k_heads = qk_heads[:, 2 * HEADS - block_heads :, :]
        straight, crossed = multiply_pairs(k_bank, "narrow")
        nc.vector.tensor_copy(out=k_heads[:, :, ROT:], in_=k_bank[:, :, ROT:])
        add_pairs(k_heads, straight, crossed)
        store(1, COLUMN_GROUPS - 1, 1)
        v_cols = slice((COLUMN_GROUPS - 1) * BLOCK, COLUMN_GROUPS * BLOCK)
        nc.scalar.copy(out=result[:, 2, v_cols], in_=acc[WIDE_BANKS][:, BLOCK:])
        nc.scalar.dma_start(out=outs[2][:, v_cols], in_=result[:, 2, v_cols])
